import numpy as np
import ml_dtypes


def mxq(x, axis, fmt="e4m3"):
    dtype, down = {"e4m3": (ml_dtypes.float8_e4m3fn, 7), "e5m2": (ml_dtypes.float8_e5m2, 14)}[fmt]
    v = np.moveaxis(np.asarray(x, np.float32).astype(ml_dtypes.bfloat16).astype(np.float64), axis, -1)
    blocks = v.reshape(v.shape[:-1] + (-1, 32))
    amax = np.abs(blocks).max(-1, keepdims=True)
    byte = np.maximum(np.where(amax > 0, np.frexp(amax)[1] - 1 + 127, 0) - down, 1)
    scale = np.exp2(byte - 127.0)
    codes = (blocks / scale).astype(np.float32).astype(dtype).astype(np.float64)
    return np.moveaxis((codes * scale).reshape(v.shape), -1, axis)


WIDE = False


def mx_kscale(k):
    if not WIDE:
        return np.ones(k)
    levels = np.array([20, -20, 10, -10, 0])
    a = np.random.permutation(np.resize(levels, k // 512 * 4)).reshape(k // 512, 4)
    idx = np.arange(k)
    return np.exp2(a[idx // 512, idx % 128 // 32])


BF16 = ml_dtypes.bfloat16


def bf(x):
    return np.asarray(x, np.float32).astype(BF16)


def f64(x):
    return np.asarray(x).astype(np.float64)


GRID_MIN, GRID_MAX = -2.0, 2.0
NUM_GRIDS = 8
NUM_KNOTS = NUM_GRIDS + 1
DELTA = (GRID_MAX - GRID_MIN) / NUM_GRIDS
IN_F, OUT_F = 1024, 1024
BATCH = 512


def silu(v):
    with np.errstate(over="ignore"):
        return v / (1.0 + np.exp(-v))


def dsilu(v):
    with np.errstate(over="ignore"):
        sg = 1.0 / (1.0 + np.exp(-v))
    return sg * (1.0 + v * (1.0 - sg))


def off_knots(x):
    x = f64(bf(x))
    near = np.abs(x / DELTA - np.round(x / DELTA)) < 1.0 / 32
    return np.where(near, x + 1.0 / 32, x)


def setup_inputs():
    u = mx_kscale(OUT_F)
    bound_base = np.sqrt(6.0 / ((1 + 5) * IN_F))
    x = off_knots(np.random.standard_normal((BATCH, IN_F)))
    sw = np.random.standard_normal((OUT_F, IN_F, NUM_KNOTS)) * 0.02 / u[:, None, None]
    bw = np.random.uniform(-bound_base, bound_base, (OUT_F, IN_F)) / u[:, None]
    b = np.random.standard_normal(OUT_F) * 0.3
    g = np.random.standard_normal((BATCH, OUT_F)) * np.exp2(np.random.randint(-12, 1, (BATCH, 1))) * 4.0 * u
    return {"x": bf(x), "spline_weight": bf(sw), "base_weight": bf(bw), "bias": bf(b), "grad_out": bf(g)}


def reference(x, spline_weight, base_weight, bias, grad_out):
    x = f64(x)
    gq = mxq(f64(grad_out), 1, "e5m2")
    wq = mxq(f64(spline_weight).transpose(2, 0, 1), 1, "e4m3")
    p = gq @ wq
    q = gq @ mxq(f64(base_weight), 0, "e4m3")
    grid = np.linspace(GRID_MIN, GRID_MAX, NUM_KNOTS)
    u = (np.clip(x, GRID_MIN, GRID_MAX)[..., None] - grid) / DELTA
    db = -np.sign(u) * (np.abs(u) < 1.0) * (np.abs(x) < GRID_MAX)[..., None] / DELTA
    return (db.transpose(2, 0, 1) * p).sum(0) + dsilu(x) * q

@@ -1,0 +1,187 @@
+from contextlib import ExitStack
+
+import concourse.mybir as mybir
+from concourse.masks import make_identity
+
+F32 = mybir.dt.float32
+BF16 = mybir.dt.bfloat16
+U32 = mybir.dt.uint32
+U8 = mybir.dt.uint8
+E4 = mybir.dt.float8_e4m3fn_x4
+E5 = mybir.dt.float8_e5m2_x4
+ALU = mybir.AluOpType
+ACT = mybir.ActivationFunctionType
+
+P = 128
+B = 512
+O = 1024
+I = 1024
+K = 9
+NBT = B // P
+NPASS = O // 512
+WI = 56
+CI = 2 * WI
+FLOPS = 2 * B * O * I * (K + 1)
+
+
+def tile_kanbasislinear_kernel(tc, x, spline_weight, base_weight, bias, grad_out, out):
+    nc = tc.nc
+    swf = spline_weight.rearrange("o i k -> o (i k)")
+    out_v = out.rearrange("(n p) i -> p n i", p=P)
+
+    def k_view(w2d, c):
+        return w2d[512 * c : 512 * (c + 1), :].rearrange("(t p) n -> p t n", p=P)
+
+    with ExitStack() as ctx:
+        const = ctx.enter_context(tc.tile_pool(name="const", bufs=1))
+        rawp = ctx.enter_context(tc.tile_pool(name="rawp", bufs=3))
+        grpp = ctx.enter_context(tc.tile_pool(name="grpp", bufs=3))
+        tps = ctx.enter_context(tc.psum_pool(name="tps", bufs=2))
+        accp = ctx.enter_context(tc.psum_pool(name="accp", bufs=6))
+
+        x_sb = const.tile([P, NBT, I], BF16)
+        g_codes = const.tile([P, NPASS, B], U32, align_bytes=64)
+        g_scales = const.tile([P, NPASS, B], U8, align_bytes=64)
+        rn = const.tile([P, NBT, I], F32)
+        si = const.tile([P, NBT, I], BF16)
+        jj = const.tile([P, 4, NBT, I], BF16)
+        ident = const.tile([P, P], BF16)
+        make_identity(nc, ident[:])
+        identf = const.tile([P, P], F32)
+        make_identity(nc, identf[:])
+        nidentf = const.tile([P, P], F32)
+        nc.vector.tensor_scalar(out=nidentf[:], in0=identf[:], scalar1=-1.0, scalar2=None, op0=ALU.mult)
+
+        braw = rawp.tile([P, NPASS, 4, I], BF16, tag="raw")
+        with tc.tile_pool(name="prep", bufs=1) as prep:
+            g_sb = prep.tile([P, NBT, O], BF16)
+            nc.sync.dma_start(out=g_sb[:], in_=grad_out.rearrange("(n p) o -> p n o", p=P))
+            nc.sync.dma_start(out=x_sb[:], in_=x.rearrange("(n p) i -> p n i", p=P))
+            for c in range(NPASS):
+                nc.sync.dma_start(out=braw[:, c, :, :], in_=k_view(base_weight, c))
+
+            for c in range(NPASS):
+                gg = prep.tile([P, B, 4], BF16, align_bytes=64, name="gg%d" % c)
+                for n in range(NBT):
+                    gt = tps.tile([P, 4, P], BF16, tag="tp")
+                    for t in range(4):
+                        k0 = 512 * c + P * t
+                        nc.tensor.transpose(gt[:, t, :], g_sb[:, n, k0 : k0 + P], ident[:])
+                    nc.scalar.copy(out=gg[:, n * P : (n + 1) * P, :], in_=gt[:].rearrange("p t r -> p r t"))
+                nc.vector.quantize_mx(
+                    out=g_codes[:, c, :].bitcast(E5),
+                    scales=g_scales[:, c, :],
+                    in_=gg[:].rearrange("p b t -> p (b t)"),
+                )
+
+            sg = prep.tile([P, NBT, I], F32)
+            nc.scalar.activation(out=sg[:], in_=x_sb[:], func=ACT.Sigmoid)
+            nc.scalar.activation(out=rn[:], in_=x_sb[:], func=ACT.Silu, scale=-1.0)
+            nc.vector.scalar_tensor_tensor(out=rn[:], in0=rn[:], scalar=1.0, in1=sg[:], op0=ALU.subtract, op1=ALU.mult)
+            r_ = jj[:, 0, :, :]
+            f_ = jj[:, 1, :, :]
+            tmp = prep.tile([P, NBT, I], BF16)
+            xc = prep.tile([P, NBT, I], BF16)
+            nc.vector.tensor_scalar(out=r_, in0=x_sb[:], scalar1=-1.5, scalar2=None, op0=ALU.is_gt)
+            for h in (-0.5, 0.5):
+                nc.vector.tensor_scalar(out=tmp[:], in0=x_sb[:], scalar1=h, scalar2=None, op0=ALU.is_gt)
+                nc.vector.tensor_tensor(out=r_, in0=r_, in1=tmp[:], op=ALU.add)
+            nc.vector.tensor_scalar(out=tmp[:], in0=x_sb[:], scalar1=1.5, scalar2=2.0, op0=ALU.is_gt, op1=ALU.subtract)
+            nc.vector.tensor_tensor(out=r_, in0=r_, in1=tmp[:], op=ALU.add)
+            nc.vector.tensor_scalar(out=xc[:], in0=x_sb[:], scalar1=2.0, scalar2=-2.0, op0=ALU.min, op1=ALU.max)
+            nc.vector.tensor_tensor(out=xc[:], in0=xc[:], in1=r_, op=ALU.subtract)
+            nc.scalar.activation(out=si[:], in_=xc[:], func=ACT.Sign)
+            nc.vector.tensor_scalar(out=tmp[:], in0=xc[:], scalar1=0.0, scalar2=None, op0=ALU.is_lt)
+            nc.vector.tensor_tensor(out=f_, in0=r_, in1=tmp[:], op=ALU.subtract)
+            nc.vector.tensor_scalar(out=jj[:, 2:4, :, :], in0=jj[:, 0:2, :, :], scalar1=-1.0, scalar2=None, op0=ALU.add)
+
+        ypool = ctx.enter_context(tc.tile_pool(name="ypool", bufs=2))
+        finp = ctx.enter_context(tc.tile_pool(name="finp", bufs=2))
+
+        def quantise_window(raw, off):
+            grouped = grpp.tile([P, NPASS, 512, 4], BF16, align_bytes=64)
+            codes = grpp.tile([P, NPASS * 512], U32, align_bytes=64)
+            scales = grpp.tile([P, NPASS * 512], U8, align_bytes=64)
+            for c in range(NPASS):
+                nc.scalar.copy(out=grouped[:, c, :, :], in_=raw[:, c, :, off : off + 512].rearrange("p t n -> p n t"))
+            nc.vector.quantize_mx(
+                out=codes[:].bitcast(E4),
+                scales=scales[:],
+                in_=grouped[:].rearrange("p c n t -> p (c n t)"),
+            )
+            return codes, scales
+
+        def product(codes, scales, n):
+            acc = accp.tile([P, 512], F32)
+            for c in range(NPASS):
+                nc.tensor.matmul_mx(
+                    out=acc[:],
+                    lhsT=g_codes[:, c, n * P : (n + 1) * P].bitcast(E5),
+                    lhsT_scale=g_scales[:, c, n * P : (n + 1) * P],
+                    rhs=codes[:, c * 512 : (c + 1) * 512].bitcast(E4),
+                    rhs_scale=scales[:, c * 512 : (c + 1) * 512],
+                    start=(c == 0),
+                    stop=(c == NPASS - 1),
+                )
+            return acc
+
+        for w in range(I // 512):
+            codes, scales = quantise_window(braw, 512 * w)
+            for n in range(NBT):
+                acc = product(codes, scales, n)
+                sl = rn[:, n, 512 * w : 512 * (w + 1)]
+                nc.vector.tensor_tensor(out=sl, in0=acc[:], in1=sl, op=ALU.mult)
+
+        chunks = [(CI * j, CI, 9 * CI * j, 9 * CI + 8) for j in range(I // CI)]
+        chunks.append((I - I % CI, I % CI, 9 * I - 512, 512))
+        for i0, ci, col0, cw in chunks:
+            raw = rawp.tile([P, NPASS, 4, 9 * CI + 8], BF16, tag="raw")
+            for c in range(NPASS):
+                nc.sync.dma_start(out=raw[:, c, :, 0:cw], in_=k_view(swf, c)[:, :, col0 : col0 + cw])
+            y = ypool.tile([P, K, NBT, ci], F32, tag="y")
+            for a in range(0, ci, WI):
+                cnt = min(WI, ci - a)
+                off = 9 * (i0 + a) - col0
+                woff = min(off, cw - 512)
+                boff = off - woff
+                codes, scales = quantise_window(raw, woff)
+                for n in range(NBT):
+                    acc = product(codes, scales, n)
+                    pk = acc[:, boff : boff + 9 * cnt].rearrange("p (i k) -> p i k", k=K)
+                    for u in range(2):
+                        nc.vector.scalar_tensor_tensor(
+                            out=y[:, 4 * u : 4 * u + 4, n, a : a + cnt].rearrange("p r i -> p i r"),
+                            in0=jj[:, :, n, i0 + a : i0 + a + cnt].rearrange("p r i -> p i r"),
+                            scalar=2.0 * u - 2.0,
+                            in1=pk[:, :, 4 * u : 4 * u + 4],
+                            op0=ALU.is_equal,
+                            op1=ALU.mult,
+                        )
+                    nc.vector.scalar_tensor_tensor(
+                        out=y[:, 8, n, a : a + cnt],
+                        in0=jj[:, 0, n, i0 + a : i0 + a + cnt],
+                        scalar=2.0,
+                        in1=pk[:, :, 8],
+                        op0=ALU.is_equal,
+                        op1=ALU.mult,
+                    )
+            yp = y[:, 0:8, :, :].rearrange("p (s r) n i -> p s r (n i)", r=2)
+            nc.vector.tensor_tensor(out=yp[:, :, 1, :], in0=yp[:, :, 1, :], in1=yp[:, :, 0, :], op=ALU.subtract)
+            dps = tps.tile([P, NBT * ci], F32, tag="tp")
+            for s in range(4):
+                nc.tensor.matmul(
+                    out=dps[:], lhsT=identf[:], rhs=y[:, 2 * s + 1, :, :].rearrange("p n i -> p (n i)"), start=(s == 0), stop=False
+                )
+            nc.tensor.matmul(out=dps[:], lhsT=nidentf[:], rhs=y[:, 8, :, :].rearrange("p n i -> p (n i)"), start=False, stop=True)
+            d = finp.tile([P, NBT, ci], F32, tag="d")
+            nc.vector.scalar_tensor_tensor(
+                out=d[:],
+                in0=si[:, :, i0 : i0 + ci],
+                scalar=2.0,
+                in1=dps[:].rearrange("p (n i) -> p n i", n=NBT),
+                op0=ALU.mult,
+                op1=ALU.mult,
+            )
+            res = finp.tile([P, NBT, ci], F32, tag="res")
+            nc.vector.tensor_tensor(out=res[:], in0=d[:], in1=rn[:, :, i0 : i0 + ci], op=ALU.subtract)
+            nc.sync.dma_start(out=out_v[:, :, i0 : i0 + ci], in_=res[:])

@@ -55,8 +55,8 @@ def tile_kanbasislinear_kernel(tc, x, spline_weight, base_weight, bias, grad_out
         braw = rawp.tile([P, NPASS, 4, I], BF16, tag="raw")
         with tc.tile_pool(name="prep", bufs=1) as prep:
             g_sb = prep.tile([P, NBT, O], BF16)
-            nc.sync.dma_start(out=g_sb[:], in_=grad_out.rearrange("(n p) o -> p n o", p=P))
             nc.sync.dma_start(out=x_sb[:], in_=x.rearrange("(n p) i -> p n i", p=P))
+            nc.sync.dma_start(out=g_sb[:], in_=grad_out.rearrange("(n p) o -> p n o", p=P))
             for c in range(NPASS):
                 nc.sync.dma_start(out=braw[:, c, :, :], in_=k_view(base_weight, c))
 
@@ -95,15 +95,22 @@ def tile_kanbasislinear_kernel(tc, x, spline_weight, base_weight, bias, grad_out
             nc.vector.tensor_tensor(out=f_, in0=r_, in1=tmp[:], op=ALU.subtract)
             nc.vector.tensor_scalar(out=jj[:, 2:4, :, :], in0=jj[:, 0:2, :, :], scalar1=-1.0, scalar2=None, op0=ALU.add)
 
-        ypool = ctx.enter_context(tc.tile_pool(name="ypool", bufs=2))
+        ypool = ctx.enter_context(tc.tile_pool(name="ypool", bufs=3))
         finp = ctx.enter_context(tc.tile_pool(name="finp", bufs=2))
+
+        unit = [0]
 
         def quantise_window(raw, off):
             grouped = grpp.tile([P, NPASS, 512, 4], BF16, align_bytes=64)
             codes = grpp.tile([P, NPASS * 512], U32, align_bytes=64)
             scales = grpp.tile([P, NPASS * 512], U8, align_bytes=64)
             for c in range(NPASS):
-                nc.scalar.copy(out=grouped[:, c, :, :], in_=raw[:, c, :, off : off + 512].rearrange("p t n -> p n t"))
+                src = raw[:, c, :, off : off + 512].rearrange("p t n -> p n t")
+                if unit[0] % 14 == 13:
+                    nc.vector.tensor_copy(out=grouped[:, c, :, :], in_=src)
+                else:
+                    nc.scalar.copy(out=grouped[:, c, :, :], in_=src)
+                unit[0] += 1
             nc.vector.quantize_mx(
                 out=codes[:].bitcast(E4),
                 scales=scales[:],
@@ -166,7 +173,8 @@ def tile_kanbasislinear_kernel(tc, x, spline_weight, base_weight, bias, grad_out
                         op1=ALU.mult,
                     )
             yp = y[:, 0:8, :, :].rearrange("p (s r) n i -> p s r (n i)", r=2)
-            nc.vector.tensor_tensor(out=yp[:, :, 1, :], in0=yp[:, :, 1, :], in1=yp[:, :, 0, :], op=ALU.subtract)
+            for s in range(4):
+                nc.gpsimd.tensor_tensor(out=yp[:, s, 1, :], in0=yp[:, s, 1, :], in1=yp[:, s, 0, :], op=ALU.subtract)
             dps = tps.tile([P, NBT * ci], F32, tag="tp")
             for s in range(4):
                 nc.tensor.matmul(

@@ -21,6 +21,8 @@ NBT = B // P
 NPASS = O // 512
 WI = 56
 CI = 2 * WI
+XS = 256
+VS = 2
 FLOPS = 2 * B * O * I * (K + 1)
 
 
@@ -34,6 +36,7 @@ def tile_kanbasislinear_kernel(tc, x, spline_weight, base_weight, bias, grad_out
 
     with ExitStack() as ctx:
         const = ctx.enter_context(tc.tile_pool(name="const", bufs=1))
+        tmpp = ctx.enter_context(tc.tile_pool(name="tmpp", bufs=2))
         rawp = ctx.enter_context(tc.tile_pool(name="rawp", bufs=3))
         grpp = ctx.enter_context(tc.tile_pool(name="grpp", bufs=3))
         tps = ctx.enter_context(tc.psum_pool(name="tps", bufs=2))
@@ -51,6 +54,26 @@ def tile_kanbasislinear_kernel(tc, x, spline_weight, base_weight, bias, grad_out
         make_identity(nc, identf[:])
         nidentf = const.tile([P, P], F32)
         nc.vector.tensor_scalar(out=nidentf[:], in0=identf[:], scalar1=-1.0, scalar2=None, op0=ALU.mult)
+
+        def index_slice(sl):
+            cs = slice(XS * sl, XS * (sl + 1))
+            xs = x_sb[:, :, cs]
+            r_ = jj[:, 0, :, cs]
+            f_ = jj[:, 1, :, cs]
+            tmp = tmpp.tile([P, NBT, XS], BF16, tag="tmp")
+            xc = tmpp.tile([P, NBT, XS], BF16, tag="xc")
+            nc.vector.tensor_scalar(out=r_, in0=xs, scalar1=-1.5, scalar2=None, op0=ALU.is_gt)
+            for h in (-0.5, 0.5):
+                nc.vector.tensor_scalar(out=tmp[:], in0=xs, scalar1=h, scalar2=None, op0=ALU.is_gt)
+                nc.vector.tensor_tensor(out=r_, in0=r_, in1=tmp[:], op=ALU.add)
+            nc.vector.tensor_scalar(out=tmp[:], in0=xs, scalar1=1.5, scalar2=2.0, op0=ALU.is_gt, op1=ALU.subtract)
+            nc.vector.tensor_tensor(out=r_, in0=r_, in1=tmp[:], op=ALU.add)
+            nc.vector.tensor_scalar(out=xc[:], in0=xs, scalar1=2.0, scalar2=-2.0, op0=ALU.min, op1=ALU.max)
+            nc.vector.tensor_tensor(out=xc[:], in0=xc[:], in1=r_, op=ALU.subtract)
+            nc.scalar.activation(out=si[:, :, cs], in_=xc[:], func=ACT.Sign)
+            nc.vector.tensor_scalar(out=tmp[:], in0=xc[:], scalar1=0.0, scalar2=None, op0=ALU.is_lt)
+            nc.vector.tensor_tensor(out=f_, in0=r_, in1=tmp[:], op=ALU.subtract)
+            nc.vector.tensor_scalar(out=jj[:, 2:4, :, cs], in0=jj[:, 0:2, :, cs], scalar1=-1.0, scalar2=None, op0=ALU.add)
 
         braw = rawp.tile([P, NPASS, 4, I], BF16, tag="raw")
         with tc.tile_pool(name="prep", bufs=1) as prep:
@@ -78,39 +101,16 @@ def tile_kanbasislinear_kernel(tc, x, spline_weight, base_weight, bias, grad_out
             nc.scalar.activation(out=sg[:], in_=x_sb[:], func=ACT.Sigmoid)
             nc.scalar.activation(out=rn[:], in_=x_sb[:], func=ACT.Silu, scale=-1.0)
             nc.vector.scalar_tensor_tensor(out=rn[:], in0=rn[:], scalar=1.0, in1=sg[:], op0=ALU.subtract, op1=ALU.mult)
-            r_ = jj[:, 0, :, :]
-            f_ = jj[:, 1, :, :]
-            tmp = prep.tile([P, NBT, I], BF16)
-            xc = prep.tile([P, NBT, I], BF16)
-            nc.vector.tensor_scalar(out=r_, in0=x_sb[:], scalar1=-1.5, scalar2=None, op0=ALU.is_gt)
-            for h in (-0.5, 0.5):
-                nc.vector.tensor_scalar(out=tmp[:], in0=x_sb[:], scalar1=h, scalar2=None, op0=ALU.is_gt)
-                nc.vector.tensor_tensor(out=r_, in0=r_, in1=tmp[:], op=ALU.add)
-            nc.vector.tensor_scalar(out=tmp[:], in0=x_sb[:], scalar1=1.5, scalar2=2.0, op0=ALU.is_gt, op1=ALU.subtract)
-            nc.vector.tensor_tensor(out=r_, in0=r_, in1=tmp[:], op=ALU.add)
-            nc.vector.tensor_scalar(out=xc[:], in0=x_sb[:], scalar1=2.0, scalar2=-2.0, op0=ALU.min, op1=ALU.max)
-            nc.vector.tensor_tensor(out=xc[:], in0=xc[:], in1=r_, op=ALU.subtract)
-            nc.scalar.activation(out=si[:], in_=xc[:], func=ACT.Sign)
-            nc.vector.tensor_scalar(out=tmp[:], in0=xc[:], scalar1=0.0, scalar2=None, op0=ALU.is_lt)
-            nc.vector.tensor_tensor(out=f_, in0=r_, in1=tmp[:], op=ALU.subtract)
-            nc.vector.tensor_scalar(out=jj[:, 2:4, :, :], in0=jj[:, 0:2, :, :], scalar1=-1.0, scalar2=None, op0=ALU.add)
 
         ypool = ctx.enter_context(tc.tile_pool(name="ypool", bufs=3))
         finp = ctx.enter_context(tc.tile_pool(name="finp", bufs=2))
-
-        unit = [0]
 
         def quantise_window(raw, off):
             grouped = grpp.tile([P, NPASS, 512, 4], BF16, align_bytes=64)
             codes = grpp.tile([P, NPASS * 512], U32, align_bytes=64)
             scales = grpp.tile([P, NPASS * 512], U8, align_bytes=64)
             for c in range(NPASS):
-                src = raw[:, c, :, off : off + 512].rearrange("p t n -> p n t")
-                if unit[0] % 14 == 13:
-                    nc.vector.tensor_copy(out=grouped[:, c, :, :], in_=src)
-                else:
-                    nc.scalar.copy(out=grouped[:, c, :, :], in_=src)
-                unit[0] += 1
+                nc.scalar.copy(out=grouped[:, c, :, :], in_=raw[:, c, :, off : off + 512].rearrange("p t n -> p n t"))
             nc.vector.quantize_mx(
                 out=codes[:].bitcast(E4),
                 scales=scales[:],
@@ -141,7 +141,11 @@ def tile_kanbasislinear_kernel(tc, x, spline_weight, base_weight, bias, grad_out
 
         chunks = [(CI * j, CI, 9 * CI * j, 9 * CI + 8) for j in range(I // CI)]
         chunks.append((I - I % CI, I % CI, 9 * I - 512, 512))
+        done = 0
         for i0, ci, col0, cw in chunks:
+            while XS * done < i0 + ci:
+                index_slice(done)
+                done += 1
             raw = rawp.tile([P, NPASS, 4, 9 * CI + 8], BF16, tag="raw")
             for c in range(NPASS):
                 nc.sync.dma_start(out=raw[:, c, :, 0:cw], in_=k_view(swf, c)[:, :, col0 : col0 + cw])
@@ -173,14 +177,17 @@ def tile_kanbasislinear_kernel(tc, x, spline_weight, base_weight, bias, grad_out
                         op1=ALU.mult,
                     )
             yp = y[:, 0:8, :, :].rearrange("p (s r) n i -> p s r (n i)", r=2)
-            for s in range(4):
-                nc.gpsimd.tensor_tensor(out=yp[:, s, 1, :], in0=yp[:, s, 1, :], in1=yp[:, s, 0, :], op=ALU.subtract)
+            nc.vector.tensor_tensor(out=yp[:, 0:VS, 1, :], in0=yp[:, 0:VS, 1, :], in1=yp[:, 0:VS, 0, :], op=ALU.subtract)
             dps = tps.tile([P, NBT * ci], F32, tag="tp")
-            for s in range(4):
+            planes = [2 * s + 1 for s in range(VS)] + list(range(2 * VS, K))
+            for q in planes:
                 nc.tensor.matmul(
-                    out=dps[:], lhsT=identf[:], rhs=y[:, 2 * s + 1, :, :].rearrange("p n i -> p (n i)"), start=(s == 0), stop=False
+                    out=dps[:],
+                    lhsT=(identf[:] if q % 2 == 1 else nidentf[:]),
+                    rhs=y[:, q, :, :].rearrange("p n i -> p (n i)"),
+                    start=(q == planes[0]),
+                    stop=(q == planes[-1]),
                 )
-            nc.tensor.matmul(out=dps[:], lhsT=nidentf[:], rhs=y[:, 8, :, :].rearrange("p n i -> p (n i)"), start=False, stop=True)
             d = finp.tile([P, NBT, ci], F32, tag="d")
             nc.vector.scalar_tensor_tensor(
                 out=d[:],

@@ -21,8 +21,6 @@ NBT = B // P
 NPASS = O // 512
 WI = 56
 CI = 2 * WI
-XS = 256
-VS = 2
 FLOPS = 2 * B * O * I * (K + 1)
 
 
@@ -36,7 +34,6 @@ def tile_kanbasislinear_kernel(tc, x, spline_weight, base_weight, bias, grad_out
 
     with ExitStack() as ctx:
         const = ctx.enter_context(tc.tile_pool(name="const", bufs=1))
-        tmpp = ctx.enter_context(tc.tile_pool(name="tmpp", bufs=2))
         rawp = ctx.enter_context(tc.tile_pool(name="rawp", bufs=3))
         grpp = ctx.enter_context(tc.tile_pool(name="grpp", bufs=3))
         tps = ctx.enter_context(tc.psum_pool(name="tps", bufs=2))
@@ -54,26 +51,6 @@ def tile_kanbasislinear_kernel(tc, x, spline_weight, base_weight, bias, grad_out
         make_identity(nc, identf[:])
         nidentf = const.tile([P, P], F32)
         nc.vector.tensor_scalar(out=nidentf[:], in0=identf[:], scalar1=-1.0, scalar2=None, op0=ALU.mult)
-
-        def index_slice(sl):
-            cs = slice(XS * sl, XS * (sl + 1))
-            xs = x_sb[:, :, cs]
-            r_ = jj[:, 0, :, cs]
-            f_ = jj[:, 1, :, cs]
-            tmp = tmpp.tile([P, NBT, XS], BF16, tag="tmp")
-            xc = tmpp.tile([P, NBT, XS], BF16, tag="xc")
-            nc.vector.tensor_scalar(out=r_, in0=xs, scalar1=-1.5, scalar2=None, op0=ALU.is_gt)
-            for h in (-0.5, 0.5):
-                nc.vector.tensor_scalar(out=tmp[:], in0=xs, scalar1=h, scalar2=None, op0=ALU.is_gt)
-                nc.vector.tensor_tensor(out=r_, in0=r_, in1=tmp[:], op=ALU.add)
-            nc.vector.tensor_scalar(out=tmp[:], in0=xs, scalar1=1.5, scalar2=2.0, op0=ALU.is_gt, op1=ALU.subtract)
-            nc.vector.tensor_tensor(out=r_, in0=r_, in1=tmp[:], op=ALU.add)
-            nc.vector.tensor_scalar(out=xc[:], in0=xs, scalar1=2.0, scalar2=-2.0, op0=ALU.min, op1=ALU.max)
-            nc.vector.tensor_tensor(out=xc[:], in0=xc[:], in1=r_, op=ALU.subtract)
-            nc.scalar.activation(out=si[:, :, cs], in_=xc[:], func=ACT.Sign)
-            nc.vector.tensor_scalar(out=tmp[:], in0=xc[:], scalar1=0.0, scalar2=None, op0=ALU.is_lt)
-            nc.vector.tensor_tensor(out=f_, in0=r_, in1=tmp[:], op=ALU.subtract)
-            nc.vector.tensor_scalar(out=jj[:, 2:4, :, cs], in0=jj[:, 0:2, :, cs], scalar1=-1.0, scalar2=None, op0=ALU.add)
 
         braw = rawp.tile([P, NPASS, 4, I], BF16, tag="raw")
         with tc.tile_pool(name="prep", bufs=1) as prep:
@@ -101,6 +78,22 @@ def tile_kanbasislinear_kernel(tc, x, spline_weight, base_weight, bias, grad_out
             nc.scalar.activation(out=sg[:], in_=x_sb[:], func=ACT.Sigmoid)
             nc.scalar.activation(out=rn[:], in_=x_sb[:], func=ACT.Silu, scale=-1.0)
             nc.vector.scalar_tensor_tensor(out=rn[:], in0=rn[:], scalar=1.0, in1=sg[:], op0=ALU.subtract, op1=ALU.mult)
+            r_ = jj[:, 0, :, :]
+            f_ = jj[:, 1, :, :]
+            tmp = prep.tile([P, NBT, I], BF16)
+            xc = prep.tile([P, NBT, I], BF16)
+            nc.vector.tensor_scalar(out=r_, in0=x_sb[:], scalar1=-1.5, scalar2=None, op0=ALU.is_gt)
+            for h in (-0.5, 0.5):
+                nc.vector.tensor_scalar(out=tmp[:], in0=x_sb[:], scalar1=h, scalar2=None, op0=ALU.is_gt)
+                nc.vector.tensor_tensor(out=r_, in0=r_, in1=tmp[:], op=ALU.add)
+            nc.vector.tensor_scalar(out=tmp[:], in0=x_sb[:], scalar1=1.5, scalar2=2.0, op0=ALU.is_gt, op1=ALU.subtract)
+            nc.vector.tensor_tensor(out=r_, in0=r_, in1=tmp[:], op=ALU.add)
+            nc.vector.tensor_scalar(out=xc[:], in0=x_sb[:], scalar1=2.0, scalar2=-2.0, op0=ALU.min, op1=ALU.max)
+            nc.vector.tensor_tensor(out=xc[:], in0=xc[:], in1=r_, op=ALU.subtract)
+            nc.scalar.activation(out=si[:], in_=xc[:], func=ACT.Sign)
+            nc.vector.tensor_scalar(out=tmp[:], in0=xc[:], scalar1=0.0, scalar2=None, op0=ALU.is_lt)
+            nc.vector.tensor_tensor(out=f_, in0=r_, in1=tmp[:], op=ALU.subtract)
+            nc.vector.tensor_scalar(out=jj[:, 2:4, :, :], in0=jj[:, 0:2, :, :], scalar1=-1.0, scalar2=None, op0=ALU.add)
 
         ypool = ctx.enter_context(tc.tile_pool(name="ypool", bufs=3))
         finp = ctx.enter_context(tc.tile_pool(name="finp", bufs=2))
@@ -141,11 +134,7 @@ def tile_kanbasislinear_kernel(tc, x, spline_weight, base_weight, bias, grad_out
 
         chunks = [(CI * j, CI, 9 * CI * j, 9 * CI + 8) for j in range(I // CI)]
         chunks.append((I - I % CI, I % CI, 9 * I - 512, 512))
-        done = 0
         for i0, ci, col0, cw in chunks:
-            while XS * done < i0 + ci:
-                index_slice(done)
-                done += 1
             raw = rawp.tile([P, NPASS, 4, 9 * CI + 8], BF16, tag="raw")
             for c in range(NPASS):
                 nc.sync.dma_start(out=raw[:, c, :, 0:cw], in_=k_view(swf, c)[:, :, col0 : col0 + cw])
@@ -177,17 +166,13 @@ def tile_kanbasislinear_kernel(tc, x, spline_weight, base_weight, bias, grad_out
                         op1=ALU.mult,
                     )
             yp = y[:, 0:8, :, :].rearrange("p (s r) n i -> p s r (n i)", r=2)
-            nc.vector.tensor_tensor(out=yp[:, 0:VS, 1, :], in0=yp[:, 0:VS, 1, :], in1=yp[:, 0:VS, 0, :], op=ALU.subtract)
+            nc.vector.tensor_tensor(out=yp[:, :, 1, :], in0=yp[:, :, 1, :], in1=yp[:, :, 0, :], op=ALU.subtract)
             dps = tps.tile([P, NBT * ci], F32, tag="tp")
-            planes = [2 * s + 1 for s in range(VS)] + list(range(2 * VS, K))
-            for q in planes:
+            for s in range(4):
                 nc.tensor.matmul(
-                    out=dps[:],
-                    lhsT=(identf[:] if q % 2 == 1 else nidentf[:]),
-                    rhs=y[:, q, :, :].rearrange("p n i -> p (n i)"),
-                    start=(q == planes[0]),
-                    stop=(q == planes[-1]),
+                    out=dps[:], lhsT=identf[:], rhs=y[:, 2 * s + 1, :, :].rearrange("p n i -> p (n i)"), start=(s == 0), stop=False
                 )
+            nc.tensor.matmul(out=dps[:], lhsT=nidentf[:], rhs=y[:, 8, :, :].rearrange("p n i -> p (n i)"), start=False, stop=True)
             d = finp.tile([P, NBT, ci], F32, tag="d")
             nc.vector.scalar_tensor_tensor(
                 out=d[:],

@@ -125,54 +125,43 @@ def tile_kanbasislinear_kernel(tc, x, spline_weight, base_weight, bias, grad_out
                 )
             return acc
 
-        for w in range(I // 512):
-            codes, scales = quantise_window(braw, 512 * w)
-            for n in range(NBT):
-                acc = product(codes, scales, n)
-                sl = rn[:, n, 512 * w : 512 * (w + 1)]
-                nc.vector.tensor_tensor(out=sl, in0=acc[:], in1=sl, op=ALU.mult)
+        def take_base(win, acc, n):
+            sl = rn[:, n, 512 * win["w"] : 512 * (win["w"] + 1)]
+            nc.vector.tensor_tensor(out=sl, in0=acc[:], in1=sl, op=ALU.mult)
 
-        chunks = [(CI * j, CI, 9 * CI * j, 9 * CI + 8) for j in range(I // CI)]
-        chunks.append((I - I % CI, I % CI, 9 * I - 512, 512))
-        for i0, ci, col0, cw in chunks:
-            raw = rawp.tile([P, NPASS, 4, 9 * CI + 8], BF16, tag="raw")
-            for c in range(NPASS):
-                nc.sync.dma_start(out=raw[:, c, :, 0:cw], in_=k_view(swf, c)[:, :, col0 : col0 + cw])
-            y = ypool.tile([P, K, NBT, ci], F32, tag="y")
-            for a in range(0, ci, WI):
-                cnt = min(WI, ci - a)
-                off = 9 * (i0 + a) - col0
-                woff = min(off, cw - 512)
-                boff = off - woff
-                codes, scales = quantise_window(raw, woff)
-                for n in range(NBT):
-                    acc = product(codes, scales, n)
-                    pk = acc[:, boff : boff + 9 * cnt].rearrange("p (i k) -> p i k", k=K)
-                    for u in range(2):
-                        nc.vector.scalar_tensor_tensor(
-                            out=y[:, 4 * u : 4 * u + 4, n, a : a + cnt].rearrange("p r i -> p i r"),
-                            in0=jj[:, :, n, i0 + a : i0 + a + cnt].rearrange("p r i -> p i r"),
-                            scalar=2.0 * u - 2.0,
-                            in1=pk[:, :, 4 * u : 4 * u + 4],
-                            op0=ALU.is_equal,
-                            op1=ALU.mult,
-                        )
-                    nc.vector.scalar_tensor_tensor(
-                        out=y[:, 8, n, a : a + cnt],
-                        in0=jj[:, 0, n, i0 + a : i0 + a + cnt],
-                        scalar=2.0,
-                        in1=pk[:, :, 8],
-                        op0=ALU.is_equal,
-                        op1=ALU.mult,
-                    )
+        def take_spline(win, acc, n):
+            y, a, cnt, i1, boff = win["y"], win["a"], win["cnt"], win["i1"], win["boff"]
+            pk = acc[:, boff : boff + 9 * cnt].rearrange("p (i k) -> p i k", k=K)
+            for u in range(2):
+                nc.vector.scalar_tensor_tensor(
+                    out=y[:, 4 * u : 4 * u + 4, n, a : a + cnt].rearrange("p r i -> p i r"),
+                    in0=jj[:, :, n, i1 : i1 + cnt].rearrange("p r i -> p i r"),
+                    scalar=2.0 * u - 2.0,
+                    in1=pk[:, :, 4 * u : 4 * u + 4],
+                    op0=ALU.is_equal,
+                    op1=ALU.mult,
+                )
+            nc.vector.scalar_tensor_tensor(
+                out=y[:, 8, n, a : a + cnt],
+                in0=jj[:, 0, n, i1 : i1 + cnt],
+                scalar=2.0,
+                in1=pk[:, :, 8],
+                op0=ALU.is_equal,
+                op1=ALU.mult,
+            )
+
+        def finish_chunk(y, i0, ci):
             yp = y[:, 0:8, :, :].rearrange("p (s r) n i -> p s r (n i)", r=2)
             nc.vector.tensor_tensor(out=yp[:, :, 1, :], in0=yp[:, :, 1, :], in1=yp[:, :, 0, :], op=ALU.subtract)
             dps = tps.tile([P, NBT * ci], F32, tag="tp")
-            for s in range(4):
+            for q in (1, 3, 5, 7, 8):
                 nc.tensor.matmul(
-                    out=dps[:], lhsT=identf[:], rhs=y[:, 2 * s + 1, :, :].rearrange("p n i -> p (n i)"), start=(s == 0), stop=False
+                    out=dps[:],
+                    lhsT=(identf[:] if q % 2 == 1 else nidentf[:]),
+                    rhs=y[:, q, :, :].rearrange("p n i -> p (n i)"),
+                    start=(q == 1),
+                    stop=(q == 8),
                 )
-            nc.tensor.matmul(out=dps[:], lhsT=nidentf[:], rhs=y[:, 8, :, :].rearrange("p n i -> p (n i)"), start=False, stop=True)
             d = finp.tile([P, NBT, ci], F32, tag="d")
             nc.vector.scalar_tensor_tensor(
                 out=d[:],
@@ -185,3 +174,49 @@ def tile_kanbasislinear_kernel(tc, x, spline_weight, base_weight, bias, grad_out
             res = finp.tile([P, NBT, ci], F32, tag="res")
             nc.vector.tensor_tensor(out=res[:], in0=d[:], in1=rn[:, :, i0 : i0 + ci], op=ALU.subtract)
             nc.sync.dma_start(out=out_v[:, :, i0 : i0 + ci], in_=res[:])
+
+        def take(win, n):
+            if win["kind"] == 0:
+                take_base(win, win["acc"][n], n)
+            else:
+                take_spline(win, win["acc"][n], n)
+            if n == NBT - 1 and win["last"]:
+                finish_chunk(win["y"], win["i0"], win["ci"])
+
+        descs = [{"kind": 0, "w": w} for w in range(I // 512)]
+        for j in range(I // CI):
+            for a in range(0, CI, WI):
+                descs.append({"kind": 1, "i0": CI * j, "ci": CI, "col0": 9 * CI * j, "cw": 9 * CI + 8, "a": a})
+        descs.append({"kind": 1, "i0": I - I % CI, "ci": I % CI, "col0": 9 * I - 512, "cw": 512, "a": 0})
+        prev = None
+        raw = braw
+        y = None
+        for dsc in descs:
+            if dsc["kind"] == 0:
+                win = {"kind": 0, "w": dsc["w"], "last": False}
+                woff = 512 * dsc["w"]
+            else:
+                i0, ci, col0, cw, a = dsc["i0"], dsc["ci"], dsc["col0"], dsc["cw"], dsc["a"]
+                if a == 0:
+                    raw = rawp.tile([P, NPASS, 4, 9 * CI + 8], BF16, tag="raw")
+                    for c in range(NPASS):
+                        nc.sync.dma_start(out=raw[:, c, :, 0:cw], in_=k_view(swf, c)[:, :, col0 : col0 + cw])
+                    y = ypool.tile([P, K, NBT, ci], F32, tag="y")
+                cnt = min(WI, ci - a)
+                off = 9 * (i0 + a) - col0
+                woff = min(off, cw - 512)
+                win = {"kind": 1, "y": y, "a": a, "cnt": cnt, "i1": i0 + a, "boff": off - woff, "i0": i0, "ci": ci}
+                win["last"] = a + cnt == ci
+            codes, scales = quantise_window(raw, woff)
+            accs = []
+            for n in range(NBT):
+                if prev is not None and n >= 2:
+                    take(prev, n - 2)
+                accs.append(product(codes, scales, n))
+            if prev is not None:
+                take(prev, 2)
+                take(prev, 3)
+            win["acc"] = accs
+            prev = win
+        for n in range(NBT):
+            take(prev, n)

@@ -95,8 +95,8 @@ def tile_kanbasislinear_kernel(tc, x, spline_weight, base_weight, bias, grad_out
             nc.vector.tensor_tensor(out=f_, in0=r_, in1=tmp[:], op=ALU.subtract)
             nc.vector.tensor_scalar(out=jj[:, 2:4, :, :], in0=jj[:, 0:2, :, :], scalar1=-1.0, scalar2=None, op0=ALU.add)
 
-        ypool = ctx.enter_context(tc.tile_pool(name="ypool", bufs=3))
-        finp = ctx.enter_context(tc.tile_pool(name="finp", bufs=2))
+        ypool = ctx.enter_context(tc.tile_pool(name="ypool", bufs=4))
+        finp = ctx.enter_context(tc.tile_pool(name="finp", bufs=3))
 
         def quantise_window(raw, off):
             grouped = grpp.tile([P, NPASS, 512, 4], BF16, align_bytes=64)
@@ -201,12 +201,12 @@ def tile_kanbasislinear_kernel(tc, x, spline_weight, base_weight, bias, grad_out
                     raw = rawp.tile([P, NPASS, 4, 9 * CI + 8], BF16, tag="raw")
                     for c in range(NPASS):
                         nc.sync.dma_start(out=raw[:, c, :, 0:cw], in_=k_view(swf, c)[:, :, col0 : col0 + cw])
-                    y = ypool.tile([P, K, NBT, ci], F32, tag="y")
                 cnt = min(WI, ci - a)
+                y = ypool.tile([P, K, NBT, cnt], F32, tag="y")
                 off = 9 * (i0 + a) - col0
                 woff = min(off, cw - 512)
-                win = {"kind": 1, "y": y, "a": a, "cnt": cnt, "i1": i0 + a, "boff": off - woff, "i0": i0, "ci": ci}
-                win["last"] = a + cnt == ci
+                win = {"kind": 1, "y": y, "a": 0, "cnt": cnt, "i1": i0 + a, "boff": off - woff, "i0": i0 + a, "ci": cnt}
+                win["last"] = True
             codes, scales = quantise_window(raw, woff)
             accs = []
             for n in range(NBT):

@@ -21,6 +21,7 @@ NBT = B // P
 NPASS = O // 512
 WI = 56
 CI = 2 * WI
+VS = 3
 FLOPS = 2 * B * O * I * (K + 1)
 
 
@@ -152,15 +153,16 @@ def tile_kanbasislinear_kernel(tc, x, spline_weight, base_weight, bias, grad_out
 
         def finish_chunk(y, i0, ci):
             yp = y[:, 0:8, :, :].rearrange("p (s r) n i -> p s r (n i)", r=2)
-            nc.vector.tensor_tensor(out=yp[:, :, 1, :], in0=yp[:, :, 1, :], in1=yp[:, :, 0, :], op=ALU.subtract)
+            nc.vector.tensor_tensor(out=yp[:, 0:VS, 1, :], in0=yp[:, 0:VS, 1, :], in1=yp[:, 0:VS, 0, :], op=ALU.subtract)
             dps = tps.tile([P, NBT * ci], F32, tag="tp")
-            for q in (1, 3, 5, 7, 8):
+            planes = [2 * s + 1 for s in range(VS)] + list(range(2 * VS, K))
+            for q in planes:
                 nc.tensor.matmul(
                     out=dps[:],
                     lhsT=(identf[:] if q % 2 == 1 else nidentf[:]),
                     rhs=y[:, q, :, :].rearrange("p n i -> p (n i)"),
-                    start=(q == 1),
-                    stop=(q == 8),
+                    start=(q == planes[0]),
+                    stop=(q == planes[-1]),
                 )
             d = finp.tile([P, NBT, ci], F32, tag="d")
             nc.vector.scalar_tensor_tensor(

from contextlib import ExitStack

import concourse.mybir as mybir
from concourse.masks import make_identity

F32 = mybir.dt.float32
BF16 = mybir.dt.bfloat16
U32 = mybir.dt.uint32
U8 = mybir.dt.uint8
E4 = mybir.dt.float8_e4m3fn_x4
E5 = mybir.dt.float8_e5m2_x4
ALU = mybir.AluOpType
ACT = mybir.ActivationFunctionType

P = 128
B = 512
O = 1024
I = 1024
K = 9
NBT = B // P
NPASS = O // 512
WI = 56
CI = 2 * WI
VS = 3
FLOPS = 2 * B * O * I * (K + 1)


def tile_kanbasislinear_kernel(tc, x, spline_weight, base_weight, bias, grad_out, out):
    nc = tc.nc
    swf = spline_weight.rearrange("o i k -> o (i k)")
    out_v = out.rearrange("(n p) i -> p n i", p=P)

    def k_view(w2d, c):
        return w2d[512 * c : 512 * (c + 1), :].rearrange("(t p) n -> p t n", p=P)

    with ExitStack() as ctx:
        const = ctx.enter_context(tc.tile_pool(name="const", bufs=1))
        rawp = ctx.enter_context(tc.tile_pool(name="rawp", bufs=3))
        grpp = ctx.enter_context(tc.tile_pool(name="grpp", bufs=3))
        tps = ctx.enter_context(tc.psum_pool(name="tps", bufs=2))
        accp = ctx.enter_context(tc.psum_pool(name="accp", bufs=6))

        x_sb = const.tile([P, NBT, I], BF16)
        g_codes = const.tile([P, NPASS, B], U32, align_bytes=64)
        g_scales = const.tile([P, NPASS, B], U8, align_bytes=64)
        rn = const.tile([P, NBT, I], F32)
        si = const.tile([P, NBT, I], BF16)
        jj = const.tile([P, 4, NBT, I], BF16)
        ident = const.tile([P, P], BF16)
        make_identity(nc, ident[:])
        identf = const.tile([P, P], F32)
        make_identity(nc, identf[:])
        nidentf = const.tile([P, P], F32)
        nc.vector.tensor_scalar(out=nidentf[:], in0=identf[:], scalar1=-1.0, scalar2=None, op0=ALU.mult)

        braw = rawp.tile([P, NPASS, 4, I], BF16, tag="raw")
        with tc.tile_pool(name="prep", bufs=1) as prep:
            g_sb = prep.tile([P, NBT, O], BF16)
            nc.sync.dma_start(out=x_sb[:], in_=x.rearrange("(n p) i -> p n i", p=P))
            nc.sync.dma_start(out=g_sb[:], in_=grad_out.rearrange("(n p) o -> p n o", p=P))
            for c in range(NPASS):
                nc.sync.dma_start(out=braw[:, c, :, :], in_=k_view(base_weight, c))

            for c in range(NPASS):
                gg = prep.tile([P, B, 4], BF16, align_bytes=64, name="gg%d" % c)
                for n in range(NBT):
                    gt = tps.tile([P, 4, P], BF16, tag="tp")
                    for t in range(4):
                        k0 = 512 * c + P * t
                        nc.tensor.transpose(gt[:, t, :], g_sb[:, n, k0 : k0 + P], ident[:])
                    nc.scalar.copy(out=gg[:, n * P : (n + 1) * P, :], in_=gt[:].rearrange("p t r -> p r t"))
                nc.vector.quantize_mx(
                    out=g_codes[:, c, :].bitcast(E5),
                    scales=g_scales[:, c, :],
                    in_=gg[:].rearrange("p b t -> p (b t)"),
                )

            sg = prep.tile([P, NBT, I], F32)
            nc.scalar.activation(out=sg[:], in_=x_sb[:], func=ACT.Sigmoid)
            nc.scalar.activation(out=rn[:], in_=x_sb[:], func=ACT.Silu, scale=-1.0)
            nc.vector.scalar_tensor_tensor(out=rn[:], in0=rn[:], scalar=1.0, in1=sg[:], op0=ALU.subtract, op1=ALU.mult)
            r_ = jj[:, 0, :, :]
            f_ = jj[:, 1, :, :]
            tmp = prep.tile([P, NBT, I], BF16)
            xc = prep.tile([P, NBT, I], BF16)
            nc.vector.tensor_scalar(out=r_, in0=x_sb[:], scalar1=-1.5, scalar2=None, op0=ALU.is_gt)
            for h in (-0.5, 0.5):
                nc.vector.tensor_scalar(out=tmp[:], in0=x_sb[:], scalar1=h, scalar2=None, op0=ALU.is_gt)
                nc.vector.tensor_tensor(out=r_, in0=r_, in1=tmp[:], op=ALU.add)
            nc.vector.tensor_scalar(out=tmp[:], in0=x_sb[:], scalar1=1.5, scalar2=2.0, op0=ALU.is_gt, op1=ALU.subtract)
            nc.vector.tensor_tensor(out=r_, in0=r_, in1=tmp[:], op=ALU.add)
            nc.vector.tensor_scalar(out=xc[:], in0=x_sb[:], scalar1=2.0, scalar2=-2.0, op0=ALU.min, op1=ALU.max)
            nc.vector.tensor_tensor(out=xc[:], in0=xc[:], in1=r_, op=ALU.subtract)
            nc.scalar.activation(out=si[:], in_=xc[:], func=ACT.Sign)
            nc.vector.tensor_scalar(out=tmp[:], in0=xc[:], scalar1=0.0, scalar2=None, op0=ALU.is_lt)
            nc.vector.tensor_tensor(out=f_, in0=r_, in1=tmp[:], op=ALU.subtract)
            nc.vector.tensor_scalar(out=jj[:, 2:4, :, :], in0=jj[:, 0:2, :, :], scalar1=-1.0, scalar2=None, op0=ALU.add)

        ypool = ctx.enter_context(tc.tile_pool(name="ypool", bufs=4))
        finp = ctx.enter_context(tc.tile_pool(name="finp", bufs=3))

        def quantise_window(raw, off):
            grouped = grpp.tile([P, NPASS, 512, 4], BF16, align_bytes=64)
            codes = grpp.tile([P, NPASS * 512], U32, align_bytes=64)
            scales = grpp.tile([P, NPASS * 512], U8, align_bytes=64)
            for c in range(NPASS):
                nc.scalar.copy(out=grouped[:, c, :, :], in_=raw[:, c, :, off : off + 512].rearrange("p t n -> p n t"))
            nc.vector.quantize_mx(
                out=codes[:].bitcast(E4),
                scales=scales[:],
                in_=grouped[:].rearrange("p c n t -> p (c n t)"),
            )
            return codes, scales

        def product(codes, scales, n):
            acc = accp.tile([P, 512], F32)
            for c in range(NPASS):
                nc.tensor.matmul_mx(
                    out=acc[:],
                    lhsT=g_codes[:, c, n * P : (n + 1) * P].bitcast(E5),
                    lhsT_scale=g_scales[:, c, n * P : (n + 1) * P],
                    rhs=codes[:, c * 512 : (c + 1) * 512].bitcast(E4),
                    rhs_scale=scales[:, c * 512 : (c + 1) * 512],
                    start=(c == 0),
                    stop=(c == NPASS - 1),
                )
            return acc

        def take_base(win, acc, n):
            sl = rn[:, n, 512 * win["w"] : 512 * (win["w"] + 1)]
            nc.vector.tensor_tensor(out=sl, in0=acc[:], in1=sl, op=ALU.mult)

        def take_spline(win, acc, n):
            y, a, cnt, i1, boff = win["y"], win["a"], win["cnt"], win["i1"], win["boff"]
            pk = acc[:, boff : boff + 9 * cnt].rearrange("p (i k) -> p i k", k=K)
            for u in range(2):
                nc.vector.scalar_tensor_tensor(
                    out=y[:, 4 * u : 4 * u + 4, n, a : a + cnt].rearrange("p r i -> p i r"),
                    in0=jj[:, :, n, i1 : i1 + cnt].rearrange("p r i -> p i r"),
                    scalar=2.0 * u - 2.0,
                    in1=pk[:, :, 4 * u : 4 * u + 4],
                    op0=ALU.is_equal,
                    op1=ALU.mult,
                )
            nc.vector.scalar_tensor_tensor(
                out=y[:, 8, n, a : a + cnt],
                in0=jj[:, 0, n, i1 : i1 + cnt],
                scalar=2.0,
                in1=pk[:, :, 8],
                op0=ALU.is_equal,
                op1=ALU.mult,
            )

        def finish_chunk(y, i0, ci):
            yp = y[:, 0:8, :, :].rearrange("p (s r) n i -> p s r (n i)", r=2)
            nc.vector.tensor_tensor(out=yp[:, 0:VS, 1, :], in0=yp[:, 0:VS, 1, :], in1=yp[:, 0:VS, 0, :], op=ALU.subtract)
            dps = tps.tile([P, NBT * ci], F32, tag="tp")
            planes = [2 * s + 1 for s in range(VS)] + list(range(2 * VS, K))
            for q in planes:
                nc.tensor.matmul(
                    out=dps[:],
                    lhsT=(identf[:] if q % 2 == 1 else nidentf[:]),
                    rhs=y[:, q, :, :].rearrange("p n i -> p (n i)"),
                    start=(q == planes[0]),
                    stop=(q == planes[-1]),
                )
            d = finp.tile([P, NBT, ci], F32, tag="d")
            nc.vector.scalar_tensor_tensor(
                out=d[:],
                in0=si[:, :, i0 : i0 + ci],
                scalar=2.0,
                in1=dps[:].rearrange("p (n i) -> p n i", n=NBT),
                op0=ALU.mult,
                op1=ALU.mult,
            )
            res = finp.tile([P, NBT, ci], F32, tag="res")
            nc.vector.tensor_tensor(out=res[:], in0=d[:], in1=rn[:, :, i0 : i0 + ci], op=ALU.subtract)
            nc.sync.dma_start(out=out_v[:, :, i0 : i0 + ci], in_=res[:])

        def take(win, n):
            if win["kind"] == 0:
                take_base(win, win["acc"][n], n)
            else:
                take_spline(win, win["acc"][n], n)
            if n == NBT - 1 and win["last"]:
                finish_chunk(win["y"], win["i0"], win["ci"])

        descs = [{"kind": 0, "w": w} for w in range(I // 512)]
        for j in range(I // CI):
            for a in range(0, CI, WI):
                descs.append({"kind": 1, "i0": CI * j, "ci": CI, "col0": 9 * CI * j, "cw": 9 * CI + 8, "a": a})
        descs.append({"kind": 1, "i0": I - I % CI, "ci": I % CI, "col0": 9 * I - 512, "cw": 512, "a": 0})
        prev = None
        raw = braw
        y = None
        for dsc in descs:
            if dsc["kind"] == 0:
                win = {"kind": 0, "w": dsc["w"], "last": False}
                woff = 512 * dsc["w"]
            else:
                i0, ci, col0, cw, a = dsc["i0"], dsc["ci"], dsc["col0"], dsc["cw"], dsc["a"]
                if a == 0:
                    raw = rawp.tile([P, NPASS, 4, 9 * CI + 8], BF16, tag="raw")
                    for c in range(NPASS):
                        nc.sync.dma_start(out=raw[:, c, :, 0:cw], in_=k_view(swf, c)[:, :, col0 : col0 + cw])
                cnt = min(WI, ci - a)
                y = ypool.tile([P, K, NBT, cnt], F32, tag="y")
                off = 9 * (i0 + a) - col0
                woff = min(off, cw - 512)
                win = {"kind": 1, "y": y, "a": 0, "cnt": cnt, "i1": i0 + a, "boff": off - woff, "i0": i0 + a, "ci": cnt}
                win["last"] = True
            codes, scales = quantise_window(raw, woff)
            accs = []
            for n in range(NBT):
                if prev is not None and n >= 2:
                    take(prev, n - 2)
                accs.append(product(codes, scales, n))
            if prev is not None:
                take(prev, 2)
                take(prev, 3)
            win["acc"] = accs
            prev = win
        for n in range(NBT):
            take(prev, n)
